import numpy as np
import ml_dtypes


def mxq(x, axis, fmt="e4m3"):
    dtype, down = {"e4m3": (ml_dtypes.float8_e4m3fn, 7), "e5m2": (ml_dtypes.float8_e5m2, 14)}[fmt]
    v = np.moveaxis(np.asarray(x, np.float32).astype(ml_dtypes.bfloat16).astype(np.float64), axis, -1)
    blocks = v.reshape(v.shape[:-1] + (-1, 32))
    amax = np.abs(blocks).max(-1, keepdims=True)
    byte = np.maximum(np.where(amax > 0, np.frexp(amax)[1] - 1 + 127, 0) - down, 1)
    scale = np.exp2(byte - 127.0)
    codes = (blocks / scale).astype(np.float32).astype(dtype).astype(np.float64)
    return np.moveaxis((codes * scale).reshape(v.shape), -1, axis)


WIDE = False


def mx_kscale(k):
    if not WIDE:
        return np.ones(k)
    levels = np.array([10, -10, 5, -5, 0])
    a = np.random.permutation(np.resize(levels, k // 512 * 4)).reshape(k // 512, 4)
    idx = np.arange(k)
    return np.exp2(a[idx // 512, idx % 128 // 32])


BF16 = ml_dtypes.bfloat16


def bf(x):
    return np.asarray(x, np.float32).astype(BF16)


def f64(x):
    return np.asarray(x).astype(np.float64)


B, N, D, NFF = 128, 1024, 8, 1024
KI = D * N
ALPHA = 0.95
RHO = 0.9
BETA = 1.8
TH = 1.0
P = 0.1
GAP = 0.0625


def spikes(shape):
    return (np.random.random_sample(shape) < P) * (1.0 + 0.25 * np.random.standard_normal(shape))


def setup_inputs():
    s = mx_kscale(KI).reshape(D, N)
    u = mx_kscale(NFF)
    a = bf(np.random.random_sample((B, N)))
    theta = TH + BETA * f64(a)
    d = 1.0 + 1.5 * np.random.standard_normal((B, N)) - theta
    V = bf(theta + d + GAP * np.sign(d))
    return {"FF": bf(spikes((B, NFF)) * u),
            "V": V,
            "a": a,
            "Xd": bf(spikes((D, B, N)) * s[:, None, :]),
            "W_int": bf(np.random.standard_normal((D, N, N)) * 0.8 / np.sqrt(P * KI) / s[:, :, None]),
            "W_ff": bf(np.random.standard_normal((NFF, N)) * 0.8 / np.sqrt(P * NFF) / u[:, None])}


def reference(FF, V, a, Xd, W_int, W_ff):
    FF, V, a, Xd, W_int, W_ff = f64(FF), f64(V), f64(a), f64(Xd), f64(W_int), f64(W_ff)
    theta = TH + BETA * a
    X = (V - theta > 0).astype(np.float64)
    xq = mxq(Xd.transpose(1, 0, 2).reshape(B, KI), 1, "e4m3")
    wq = mxq(W_int.reshape(KI, N), 0, "e4m3")
    I_int = xq @ wq
    I_ff = mxq(FF, 1, "e4m3") @ mxq(W_ff, 0, "e4m3")
    current = I_int + I_ff
    V_new = ALPHA * V * (1.0 - X) + current
    a_new = RHO * a + X
    return np.stack([X, V_new, a_new])

@@ -1,0 +1,151 @@
+from contextlib import ExitStack
+
+import concourse.mybir as mybir
+from concourse.masks import make_identity
+
+FP8X4 = mybir.dt.float8_e4m3fn_x4
+BF16 = mybir.dt.bfloat16
+F32 = mybir.dt.float32
+U32 = mybir.dt.uint32
+U8 = mybir.dt.uint8
+ALU = mybir.AluOpType
+
+P = 128
+N = 1024
+K_PASS = 512
+PASSES = 18
+HALF = 512
+CV = 512
+RAW_BUFS = 8
+FLOPS = 2 * 128 * 9216 * 1024
+
+
+def tile_snn_kernel(tc, FF, V, a, Xd, W_int, W_ff, out):
+    nc = tc.nc
+    w_int_rows = W_int.rearrange("d n m -> (d n) m")
+    with ExitStack() as ctx:
+        keep = ctx.enter_context(tc.tile_pool(name="keep", bufs=1))
+        rawp = ctx.enter_context(tc.tile_pool(name="rawp", bufs=RAW_BUFS))
+        grpp = ctx.enter_context(tc.tile_pool(name="grpp", bufs=3))
+        codp = ctx.enter_context(tc.tile_pool(name="codp", bufs=3))
+        psx = ctx.enter_context(tc.psum_pool(name="psx", bufs=4))
+        psa = ctx.enter_context(tc.psum_pool(name="psa", bufs=1))
+        ctx.enter_context(tc.manual_schedule())
+
+        ident = keep.tile([P, P], F32)
+        make_identity(nc, ident[:])
+
+        a_sb = keep.tile([P, N], BF16)
+        v_sb = keep.tile([P, N], BF16)
+        x_sb = keep.tile([P, 9 * N], BF16)
+        nc.sync.dma_start(out=a_sb[:], in_=a)
+        nc.sync.dma_start(out=v_sb[:], in_=V)
+        for d0 in range(0, 8, 2):
+            nc.sync.dma_start(
+                out=x_sb[:, d0 * N : (d0 + 2) * N].rearrange("b (d n) -> b d n", d=2),
+                in_=Xd[d0 : d0 + 2].rearrange("d b n -> b d n"),
+            )
+        nc.sync.dma_start(out=x_sb[:, 8 * N : 9 * N], in_=FF)
+
+        dist = keep.tile([P, N], F32)
+        spike = keep.tile([P, N], F32)
+        a_new = keep.tile([P, N], F32)
+        v_keep = keep.tile([P, N], F32)
+        v_new = keep.tile([P, N], F32)
+        nc.vector.scalar_tensor_tensor(
+            out=dist[:], in0=a_sb[:], scalar=-1.8, in1=v_sb[:], op0=ALU.mult, op1=ALU.add
+        )
+        nc.vector.tensor_single_scalar(out=spike[:], in_=dist[:], scalar=1.0, op=ALU.is_gt)
+        nc.vector.scalar_tensor_tensor(
+            out=a_new[:], in0=a_sb[:], scalar=0.9, in1=spike[:], op0=ALU.mult, op1=ALU.add
+        )
+        nc.vector.scalar_tensor_tensor(
+            out=v_keep[:], in0=dist[:], scalar=1.0, in1=v_sb[:], op0=ALU.is_le, op1=ALU.mult
+        )
+
+        x32 = x_sb[:].bitcast(F32)
+        xg = keep.tile([P, PASSES * P * 4], BF16, align_bytes=64)
+        xg32 = xg[:].bitcast(F32)
+        x_codes = keep.tile([P, PASSES * P], U32, align_bytes=64)
+        x_scales = keep.tile([P, PASSES * P], U8, align_bytes=64)
+        for bank in range(PASSES // 2):
+            xt = psx.tile([P, 2, 2, P], F32)
+            for j in range(2):
+                c = 2 * bank + j
+                for u in range(2):
+                    nc.tensor.transpose(
+                        xt[:, j, u, :], x32[:, 256 * c + u : 256 * (c + 1) : 2], ident[:]
+                    )
+            nc.scalar.copy(
+                out=xg32[:, 512 * bank : 512 * (bank + 1)].rearrange(
+                    "p (j b u) -> p j b u", j=2, u=2
+                ),
+                in_=xt[:].rearrange("p j u b -> p j b u"),
+            )
+            nc.vector.quantize_mx(
+                out=x_codes[:, 256 * bank : 256 * (bank + 1)].bitcast(FP8X4),
+                scales=x_scales[:, 256 * bank : 256 * (bank + 1)],
+                in_=xg[:, 1024 * bank : 1024 * (bank + 1)],
+            )
+
+        acc = [
+            psa.tile([P, HALF], F32, name="acc0"),
+            psa.tile([P, HALF], F32, name="acc1"),
+        ]
+
+        def regroup(copy, grouped, raw, lo, hi):
+            copy(
+                out=grouped[:, lo:hi, :].rearrange("p (c i) t -> p c t i", i=4),
+                in_=raw[:, :, lo:hi].rearrange("p t (c i) -> p c t i", i=4),
+            )
+
+        def quantise_and_multiply(c, h, grouped, codes, scales):
+            cols = slice(h * HALF, (h + 1) * HALF)
+            nc.vector.quantize_mx(
+                out=codes[:, cols].bitcast(FP8X4),
+                scales=scales[:, cols],
+                in_=grouped[:, cols, :].rearrange("p w t -> p (w t)"),
+            )
+            nc.tensor.matmul_mx(
+                out=acc[h][:],
+                lhsT=x_codes[:, P * c : P * (c + 1)].bitcast(FP8X4),
+                lhsT_scale=x_scales[:, P * c : P * (c + 1)],
+                rhs=codes[:, cols].bitcast(FP8X4),
+                rhs_scale=scales[:, cols],
+                start=(c == 0),
+                stop=(c == PASSES - 1),
+            )
+
+        prev = None
+        for c in range(PASSES):
+            rows = (
+                w_int_rows[K_PASS * c : K_PASS * (c + 1), :]
+                if c < 16
+                else W_ff[K_PASS * (c - 16) : K_PASS * (c - 15), :]
+            )
+            raw = rawp.tile([P, 4, N], BF16)
+            nc.sync.dma_start(out=raw[:], in_=rows.rearrange("(p t) w -> p t w", t=4))
+            grouped = grpp.tile([P, N, 4], BF16, align_bytes=64)
+            codes = codp.tile([P, N], U32, align_bytes=64)
+            scales = codp.tile([P, N], U8, align_bytes=64)
+            regroup(nc.vector.tensor_copy, grouped, raw, 0, CV)
+            regroup(nc.scalar.copy, grouped, raw, CV, N)
+            if prev is not None:
+                quantise_and_multiply(c - 1, 1, prev[0], prev[1], prev[2])
+            quantise_and_multiply(c, 0, grouped, codes, scales)
+            prev = (grouped, codes, scales)
+        quantise_and_multiply(PASSES - 1, 1, prev[0], prev[1], prev[2])
+
+        nc.sync.dma_start(out=out[0], in_=spike[:])
+        nc.sync.dma_start(out=out[2], in_=a_new[:])
+        for h in range(2):
+            cols = slice(h * HALF, (h + 1) * HALF)
+            nc.vector.scalar_tensor_tensor(
+                out=v_new[:, cols],
+                in0=v_keep[:, cols],
+                scalar=0.95,
+                in1=acc[h][:],
+                op0=ALU.mult,
+                op1=ALU.add,
+            )
+            nc.sync.dma_start(out=out[1][:, cols], in_=v_new[:, cols])

@@ -15,9 +15,12 @@ N = 1024
 K_PASS = 512
 PASSES = 18
 HALF = 512
-CV = 512
-RAW_BUFS = 8
 FLOPS = 2 * 128 * 9216 * 1024
+
+CV = [224,512,512,512,512,512,512,512,512,512,512,512,512,512,512,512,512,512]
+FIRST = 256
+AHEAD = 2
+X_GROUPS = [(0, 2, 4, 3, 4, 4), (2, 2, 7, 6, 7, 7), (4, 2, 10, 9, 10, 10), (6, 2, 13, 12, 13, 13), (8, 1, 15, 14, 15, 15)]
 
 
 def tile_snn_kernel(tc, FF, V, a, Xd, W_int, W_ff, out):
@@ -25,9 +28,9 @@ def tile_snn_kernel(tc, FF, V, a, Xd, W_int, W_ff, out):
     w_int_rows = W_int.rearrange("d n m -> (d n) m")
     with ExitStack() as ctx:
         keep = ctx.enter_context(tc.tile_pool(name="keep", bufs=1))
-        rawp = ctx.enter_context(tc.tile_pool(name="rawp", bufs=RAW_BUFS))
-        grpp = ctx.enter_context(tc.tile_pool(name="grpp", bufs=3))
-        codp = ctx.enter_context(tc.tile_pool(name="codp", bufs=3))
+        rawp = ctx.enter_context(tc.tile_pool(name="rawp", bufs=8))
+        grpp = ctx.enter_context(tc.tile_pool(name="grpp", bufs=4))
+        codp = ctx.enter_context(tc.tile_pool(name="codp", bufs=8))
         psx = ctx.enter_context(tc.psum_pool(name="psx", bufs=4))
         psa = ctx.enter_context(tc.psum_pool(name="psa", bufs=1))
         ctx.enter_context(tc.manual_schedule())
@@ -35,17 +38,14 @@ def tile_snn_kernel(tc, FF, V, a, Xd, W_int, W_ff, out):
         ident = keep.tile([P, P], F32)
         make_identity(nc, ident[:])
 
+        warm = keep.tile([P, 1], F32)
+        nc.scalar.copy(out=warm[:], in_=ident[:, 0:1])
+
         a_sb = keep.tile([P, N], BF16)
         v_sb = keep.tile([P, N], BF16)
         x_sb = keep.tile([P, 9 * N], BF16)
         nc.sync.dma_start(out=a_sb[:], in_=a)
         nc.sync.dma_start(out=v_sb[:], in_=V)
-        for d0 in range(0, 8, 2):
-            nc.sync.dma_start(
-                out=x_sb[:, d0 * N : (d0 + 2) * N].rearrange("b (d n) -> b d n", d=2),
-                in_=Xd[d0 : d0 + 2].rearrange("d b n -> b d n"),
-            )
-        nc.sync.dma_start(out=x_sb[:, 8 * N : 9 * N], in_=FF)
 
         dist = keep.tile([P, N], F32)
         spike = keep.tile([P, N], F32)
@@ -68,30 +68,63 @@ def tile_snn_kernel(tc, FF, V, a, Xd, W_int, W_ff, out):
         xg32 = xg[:].bitcast(F32)
         x_codes = keep.tile([P, PASSES * P], U32, align_bytes=64)
         x_scales = keep.tile([P, PASSES * P], U8, align_bytes=64)
-        for bank in range(PASSES // 2):
-            xt = psx.tile([P, 2, 2, P], F32)
-            for j in range(2):
-                c = 2 * bank + j
-                for u in range(2):
-                    nc.tensor.transpose(
-                        xt[:, j, u, :], x32[:, 256 * c + u : 256 * (c + 1) : 2], ident[:]
-                    )
-            nc.scalar.copy(
-                out=xg32[:, 512 * bank : 512 * (bank + 1)].rearrange(
-                    "p (j b u) -> p j b u", j=2, u=2
-                ),
-                in_=xt[:].rearrange("p j u b -> p j b u"),
-            )
+        x_banks = {}
+
+        def x_load(d0, nd):
+            if d0 == 8:
+                nc.sync.dma_start(out=x_sb[:, 8 * N : 9 * N], in_=FF)
+            else:
+                nc.sync.dma_start(
+                    out=x_sb[:, d0 * N : (d0 + nd) * N].rearrange("b (d n) -> b d n", d=nd),
+                    in_=Xd[d0 : d0 + nd].rearrange("d b n -> b d n"),
+                )
+
+        def x_transpose(d0, nd):
+            for d in range(d0, d0 + nd):
+                xt = psx.tile([P, 2, 2, P], F32, name="xt")
+                x_banks[d] = xt
+                for j in range(2):
+                    c = 2 * d + j
+                    for u in range(2):
+                        nc.tensor.transpose(
+                            xt[:, j, u, :], x32[:, 256 * c + u : 256 * (c + 1) : 2], ident[:]
+                        )
+
+        def x_copy(d0, nd):
+            for d in range(d0, d0 + nd):
+                nc.scalar.copy(
+                    out=xg32[:, 512 * d : 512 * (d + 1)].rearrange(
+                        "p (j b u) -> p j b u", j=2, u=2
+                    ),
+                    in_=x_banks[d][:].rearrange("p j u b -> p j b u"),
+                )
+
+        def x_quantise(d0, nd):
             nc.vector.quantize_mx(
-                out=x_codes[:, 256 * bank : 256 * (bank + 1)].bitcast(FP8X4),
-                scales=x_scales[:, 256 * bank : 256 * (bank + 1)],
-                in_=xg[:, 1024 * bank : 1024 * (bank + 1)],
+                out=x_codes[:, 256 * d0 : 256 * (d0 + nd)].bitcast(FP8X4),
+                scales=x_scales[:, 256 * d0 : 256 * (d0 + nd)],
+                in_=xg[:, 1024 * d0 : 1024 * (d0 + nd)],
             )
 
         acc = [
             psa.tile([P, HALF], F32, name="acc0"),
             psa.tile([P, HALF], F32, name="acc1"),
         ]
+        raws = {}
+
+        def w_load(c):
+            rows = (
+                w_int_rows[K_PASS * c : K_PASS * (c + 1), :]
+                if c < 16
+                else W_ff[K_PASS * (c - 16) : K_PASS * (c - 15), :]
+            ).rearrange("(p t) w -> p t w", t=4)
+            raw = rawp.tile([P, 4, N], BF16, name="raw")
+            raws[c] = raw
+            if c == 0:
+                nc.sync.dma_start(out=raw[:, :, N - FIRST : N], in_=rows[:, :, N - FIRST : N])
+                nc.sync.dma_start(out=raw[:, :, 0 : N - FIRST], in_=rows[:, :, 0 : N - FIRST])
+            else:
+                nc.sync.dma_start(out=raw[:], in_=rows)
 
         def regroup(copy, grouped, raw, lo, hi):
             copy(
@@ -99,42 +132,69 @@ def tile_snn_kernel(tc, FF, V, a, Xd, W_int, W_ff, out):
                 in_=raw[:, :, lo:hi].rearrange("p t (c i) -> p c t i", i=4),
             )
 
-        def quantise_and_multiply(c, h, grouped, codes, scales):
-            cols = slice(h * HALF, (h + 1) * HALF)
+        def quantise(work, lo, hi):
             nc.vector.quantize_mx(
-                out=codes[:, cols].bitcast(FP8X4),
-                scales=scales[:, cols],
-                in_=grouped[:, cols, :].rearrange("p w t -> p (w t)"),
+                out=work[1][:, lo:hi].bitcast(FP8X4),
+                scales=work[2][:, lo:hi],
+                in_=work[0][:, lo:hi, :].rearrange("p w t -> p (w t)"),
             )
+
+        def multiply(c, h, work):
+            cols = slice(h * HALF, (h + 1) * HALF)
             nc.tensor.matmul_mx(
                 out=acc[h][:],
                 lhsT=x_codes[:, P * c : P * (c + 1)].bitcast(FP8X4),
                 lhsT_scale=x_scales[:, P * c : P * (c + 1)],
-                rhs=codes[:, cols].bitcast(FP8X4),
-                rhs_scale=scales[:, cols],
+                rhs=work[1][:, cols].bitcast(FP8X4),
+                rhs_scale=work[2][:, cols],
                 start=(c == 0),
                 stop=(c == PASSES - 1),
             )
 
+        loaded = 0
+        x_ready = 0
+        waiting = []
+        multiplied = 0
         prev = None
         for c in range(PASSES):
-            rows = (
-                w_int_rows[K_PASS * c : K_PASS * (c + 1), :]
-                if c < 16
-                else W_ff[K_PASS * (c - 16) : K_PASS * (c - 15), :]
-            )
-            raw = rawp.tile([P, 4, N], BF16)
-            nc.sync.dma_start(out=raw[:], in_=rows.rearrange("(p t) w -> p t w", t=4))
+            while loaded < min(PASSES, c + AHEAD + 1):
+                for g in X_GROUPS:
+                    if g[2] == loaded:
+                        x_load(g[0], g[1])
+                w_load(loaded)
+                loaded += 1
+            raw = raws[c]
+            for g in X_GROUPS:
+                if g[3] == c:
+                    x_transpose(g[0], g[1])
+            for g in X_GROUPS:
+                if g[4] == c:
+                    x_copy(g[0], g[1])
             grouped = grpp.tile([P, N, 4], BF16, align_bytes=64)
             codes = codp.tile([P, N], U32, align_bytes=64)
             scales = codp.tile([P, N], U8, align_bytes=64)
-            regroup(nc.vector.tensor_copy, grouped, raw, 0, CV)
-            regroup(nc.scalar.copy, grouped, raw, CV, N)
+            if c == 0:
+                regroup(nc.scalar.copy, grouped, raw, N - FIRST, N)
+                regroup(nc.scalar.copy, grouped, raw, CV[c], N - FIRST)
+            else:
+                regroup(nc.scalar.copy, grouped, raw, CV[c], N)
+            regroup(nc.vector.tensor_copy, grouped, raw, 0, CV[c])
+            for g in X_GROUPS:
+                if g[5] == c:
+                    x_quantise(g[0], g[1])
+                    x_ready = 2 * (g[0] + g[1])
             if prev is not None:
-                quantise_and_multiply(c - 1, 1, prev[0], prev[1], prev[2])
-            quantise_and_multiply(c, 0, grouped, codes, scales)
+                quantise(prev, 0, N)
+                waiting.append((c - 1, prev))
+            while multiplied < len(waiting) and waiting[multiplied][0] < x_ready:
+                job = waiting[multiplied]
+                multiply(job[0], 0, job[1])
+                multiply(job[0], 1, job[1])
+                multiplied += 1
             prev = (grouped, codes, scales)
-        quantise_and_multiply(PASSES - 1, 1, prev[0], prev[1], prev[2])
+        for h in range(2):
+            quantise(prev, h * HALF, (h + 1) * HALF)
+            multiply(PASSES - 1, h, prev)
 
         nc.sync.dma_start(out=out[0], in_=spike[:])
         nc.sync.dma_start(out=out[2], in_=a_new[:])

@@ -17,8 +17,10 @@ PASSES = 18
 HALF = 512
 FLOPS = 2 * 128 * 9216 * 1024
 
-CV = [224,512,512,512,512,512,512,512,512,512,512,512,512,512,512,512,512,512]
+CV = [224,512,512,512,512,512,512,512,512,512,512,424,424,424,424,424,424,424]
 FIRST = 256
+VIA_PE = [11,12,13,14,15,16,17]
+PE_COLS = 256
 AHEAD = 2
 X_GROUPS = [(0, 2, 4, 3, 4, 4), (2, 2, 7, 6, 7, 7), (4, 2, 10, 9, 10, 10), (6, 2, 13, 12, 13, 13), (8, 1, 15, 14, 15, 15)]
 
@@ -33,11 +35,14 @@ def tile_snn_kernel(tc, FF, V, a, Xd, W_int, W_ff, out):
         codp = ctx.enter_context(tc.tile_pool(name="codp", bufs=8))
         psx = ctx.enter_context(tc.psum_pool(name="psx", bufs=4))
         psa = ctx.enter_context(tc.psum_pool(name="psa", bufs=1))
+        psw = ctx.enter_context(tc.psum_pool(name="psw", bufs=2))
         ctx.enter_context(tc.manual_schedule())
 
         ident = keep.tile([P, P], F32)
         make_identity(nc, ident[:])
 
+        ident_bf = keep.tile([P, P], BF16)
+        make_identity(nc, ident_bf[:])
         warm = keep.tile([P, 1], F32)
         nc.scalar.copy(out=warm[:], in_=ident[:, 0:1])
 
@@ -132,6 +137,24 @@ def tile_snn_kernel(tc, FF, V, a, Xd, W_int, W_ff, out):
                 in_=raw[:, :, lo:hi].rearrange("p t (c i) -> p c t i", i=4),
             )
 
+        banks = {}
+
+        def interleave_on_tensor_engine(k):
+            bank = psw.tile([P, 2 * PE_COLS], F32, name="bank")
+            banks[k] = bank
+            words = bank[:].rearrange("p (w u) -> p w u", u=2)
+            halves = bank[:].bitcast(BF16).rearrange("p (w t) -> p w t", t=4)
+            for u in range(2):
+                nc.tensor.matmul(
+                    out=words[:, :, u], lhsT=ident_bf[:],
+                    rhs=raws[k][:, 2 * u + 1, N - PE_COLS : N], start=True, stop=True,
+                )
+            for u in range(2):
+                nc.tensor.matmul(
+                    out=halves[:, :, 2 * u], lhsT=ident_bf[:],
+                    rhs=raws[k][:, 2 * u, N - PE_COLS : N], start=True, stop=True,
+                )
+
         def quantise(work, lo, hi):
             nc.vector.quantize_mx(
                 out=work[1][:, lo:hi].bitcast(FP8X4),
@@ -164,6 +187,8 @@ def tile_snn_kernel(tc, FF, V, a, Xd, W_int, W_ff, out):
                 w_load(loaded)
                 loaded += 1
             raw = raws[c]
+            if c + 1 in VIA_PE:
+                interleave_on_tensor_engine(c + 1)
             for g in X_GROUPS:
                 if g[3] == c:
                     x_transpose(g[0], g[1])
@@ -176,6 +201,12 @@ def tile_snn_kernel(tc, FF, V, a, Xd, W_int, W_ff, out):
             if c == 0:
                 regroup(nc.scalar.copy, grouped, raw, N - FIRST, N)
                 regroup(nc.scalar.copy, grouped, raw, CV[c], N - FIRST)
+            elif c in VIA_PE:
+                regroup(nc.scalar.copy, grouped, raw, CV[c], N - PE_COLS)
+                nc.scalar.copy(
+                    out=grouped[:, N - PE_COLS : N, :].rearrange("p w t -> p (w t)"),
+                    in_=banks[c][:].bitcast(BF16),
+                )
             else:
                 regroup(nc.scalar.copy, grouped, raw, CV[c], N)
             regroup(nc.vector.tensor_copy, grouped, raw, 0, CV[c])

@@ -17,7 +17,7 @@ PASSES = 18
 HALF = 512
 FLOPS = 2 * 128 * 9216 * 1024
 
-CV = [224,512,512,512,512,512,512,512,512,512,512,424,424,424,424,424,424,424]
+CV = [224,512,512,512,512,512,512,512,512,512,512,456,456,456,456,456,384,384]
 FIRST = 256
 VIA_PE = [11,12,13,14,15,16,17]
 PE_COLS = 256
@@ -187,8 +187,6 @@ def tile_snn_kernel(tc, FF, V, a, Xd, W_int, W_ff, out):
                 w_load(loaded)
                 loaded += 1
             raw = raws[c]
-            if c + 1 in VIA_PE:
-                interleave_on_tensor_engine(c + 1)
             for g in X_GROUPS:
                 if g[3] == c:
                     x_transpose(g[0], g[1])
@@ -222,6 +220,8 @@ def tile_snn_kernel(tc, FF, V, a, Xd, W_int, W_ff, out):
                 multiply(job[0], 0, job[1])
                 multiply(job[0], 1, job[1])
                 multiplied += 1
+            if c + 1 in VIA_PE:
+                interleave_on_tensor_engine(c + 1)
             prev = (grouped, codes, scales)
         for h in range(2):
             quantise(prev, h * HALF, (h + 1) * HALF)

@@ -17,10 +17,7 @@ PASSES = 18
 HALF = 512
 FLOPS = 2 * 128 * 9216 * 1024
 
-CV = [224,512,512,512,512,512,512,512,512,512,512,456,456,456,456,456,384,384]
-FIRST = 256
-VIA_PE = [11,12,13,14,15,16,17]
-PE_COLS = 256
+CV = [512,512,512,512,512,512,512,512,512,512,512,512,512,512,512,512,512,512]
 AHEAD = 2
 X_GROUPS = [(0, 2, 4, 3, 4, 4), (2, 2, 7, 6, 7, 7), (4, 2, 10, 9, 10, 10), (6, 2, 13, 12, 13, 13), (8, 1, 15, 14, 15, 15)]
 
@@ -35,14 +32,11 @@ def tile_snn_kernel(tc, FF, V, a, Xd, W_int, W_ff, out):
         codp = ctx.enter_context(tc.tile_pool(name="codp", bufs=8))
         psx = ctx.enter_context(tc.psum_pool(name="psx", bufs=4))
         psa = ctx.enter_context(tc.psum_pool(name="psa", bufs=1))
-        psw = ctx.enter_context(tc.psum_pool(name="psw", bufs=2))
         ctx.enter_context(tc.manual_schedule())
 
         ident = keep.tile([P, P], F32)
         make_identity(nc, ident[:])
 
-        ident_bf = keep.tile([P, P], BF16)
-        make_identity(nc, ident_bf[:])
         warm = keep.tile([P, 1], F32)
         nc.scalar.copy(out=warm[:], in_=ident[:, 0:1])
 
@@ -125,35 +119,13 @@ def tile_snn_kernel(tc, FF, V, a, Xd, W_int, W_ff, out):
             ).rearrange("(p t) w -> p t w", t=4)
             raw = rawp.tile([P, 4, N], BF16, name="raw")
             raws[c] = raw
-            if c == 0:
-                nc.sync.dma_start(out=raw[:, :, N - FIRST : N], in_=rows[:, :, N - FIRST : N])
-                nc.sync.dma_start(out=raw[:, :, 0 : N - FIRST], in_=rows[:, :, 0 : N - FIRST])
-            else:
-                nc.sync.dma_start(out=raw[:], in_=rows)
+            nc.sync.dma_start(out=raw[:], in_=rows)
 
         def regroup(copy, grouped, raw, lo, hi):
             copy(
                 out=grouped[:, lo:hi, :].rearrange("p (c i) t -> p c t i", i=4),
                 in_=raw[:, :, lo:hi].rearrange("p t (c i) -> p c t i", i=4),
             )
-
-        banks = {}
-
-        def interleave_on_tensor_engine(k):
-            bank = psw.tile([P, 2 * PE_COLS], F32, name="bank")
-            banks[k] = bank
-            words = bank[:].rearrange("p (w u) -> p w u", u=2)
-            halves = bank[:].bitcast(BF16).rearrange("p (w t) -> p w t", t=4)
-            for u in range(2):
-                nc.tensor.matmul(
-                    out=words[:, :, u], lhsT=ident_bf[:],
-                    rhs=raws[k][:, 2 * u + 1, N - PE_COLS : N], start=True, stop=True,
-                )
-            for u in range(2):
-                nc.tensor.matmul(
-                    out=halves[:, :, 2 * u], lhsT=ident_bf[:],
-                    rhs=raws[k][:, 2 * u, N - PE_COLS : N], start=True, stop=True,
-                )
 
         def quantise(work, lo, hi):
             nc.vector.quantize_mx(
@@ -196,17 +168,7 @@ def tile_snn_kernel(tc, FF, V, a, Xd, W_int, W_ff, out):
             grouped = grpp.tile([P, N, 4], BF16, align_bytes=64)
             codes = codp.tile([P, N], U32, align_bytes=64)
             scales = codp.tile([P, N], U8, align_bytes=64)
-            if c == 0:
-                regroup(nc.scalar.copy, grouped, raw, N - FIRST, N)
-                regroup(nc.scalar.copy, grouped, raw, CV[c], N - FIRST)
-            elif c in VIA_PE:
-                regroup(nc.scalar.copy, grouped, raw, CV[c], N - PE_COLS)
-                nc.scalar.copy(
-                    out=grouped[:, N - PE_COLS : N, :].rearrange("p w t -> p (w t)"),
-                    in_=banks[c][:].bitcast(BF16),
-                )
-            else:
-                regroup(nc.scalar.copy, grouped, raw, CV[c], N)
+            regroup(nc.scalar.copy, grouped, raw, CV[c], N)
             regroup(nc.vector.tensor_copy, grouped, raw, 0, CV[c])
             for g in X_GROUPS:
                 if g[5] == c:
@@ -220,8 +182,6 @@ def tile_snn_kernel(tc, FF, V, a, Xd, W_int, W_ff, out):
                 multiply(job[0], 0, job[1])
                 multiply(job[0], 1, job[1])
                 multiplied += 1
-            if c + 1 in VIA_PE:
-                interleave_on_tensor_engine(c + 1)
             prev = (grouped, codes, scales)
         for h in range(2):
             quantise(prev, h * HALF, (h + 1) * HALF)

@@ -9,6 +9,7 @@ F32 = mybir.dt.float32
 U32 = mybir.dt.uint32
 U8 = mybir.dt.uint8
 ALU = mybir.AluOpType
+ACT = mybir.ActivationFunctionType
 
 P = 128
 N = 1024
@@ -46,20 +47,20 @@ def tile_snn_kernel(tc, FF, V, a, Xd, W_int, W_ff, out):
         nc.sync.dma_start(out=a_sb[:], in_=a)
         nc.sync.dma_start(out=v_sb[:], in_=V)
 
-        dist = keep.tile([P, N], F32)
+        theta = keep.tile([P, N], F32)
         spike = keep.tile([P, N], F32)
         a_new = keep.tile([P, N], F32)
         v_keep = keep.tile([P, N], F32)
         v_new = keep.tile([P, N], F32)
-        nc.vector.scalar_tensor_tensor(
-            out=dist[:], in0=a_sb[:], scalar=-1.8, in1=v_sb[:], op0=ALU.mult, op1=ALU.add
-        )
-        nc.vector.tensor_single_scalar(out=spike[:], in_=dist[:], scalar=1.0, op=ALU.is_gt)
+        for h in range(2):
+            cols = slice(h * HALF, (h + 1) * HALF)
+            nc.scalar.activation(out=theta[:, cols], in_=a_sb[:, cols], func=ACT.Copy, scale=1.8, bias=1.0)
+            nc.vector.tensor_tensor(out=spike[:, cols], in0=v_sb[:, cols], in1=theta[:, cols], op=ALU.is_gt)
         nc.vector.scalar_tensor_tensor(
             out=a_new[:], in0=a_sb[:], scalar=0.9, in1=spike[:], op0=ALU.mult, op1=ALU.add
         )
         nc.vector.scalar_tensor_tensor(
-            out=v_keep[:], in0=dist[:], scalar=1.0, in1=v_sb[:], op0=ALU.is_le, op1=ALU.mult
+            out=v_keep[:], in0=spike[:], scalar=0.0, in1=v_sb[:], op0=ALU.is_equal, op1=ALU.mult
         )
 
         x32 = x_sb[:].bitcast(F32)
@@ -119,7 +120,11 @@ def tile_snn_kernel(tc, FF, V, a, Xd, W_int, W_ff, out):
             ).rearrange("(p t) w -> p t w", t=4)
             raw = rawp.tile([P, 4, N], BF16, name="raw")
             raws[c] = raw
-            nc.sync.dma_start(out=raw[:], in_=rows)
+            if c == 0:
+                nc.sync.dma_start(out=raw[:, :, HALF:], in_=rows[:, :, HALF:])
+                nc.sync.dma_start(out=raw[:, :, :HALF], in_=rows[:, :, :HALF])
+            else:
+                nc.sync.dma_start(out=raw[:], in_=rows)
 
         def regroup(copy, grouped, raw, lo, hi):
             copy(

@@ -18,7 +18,7 @@ PASSES = 18
 HALF = 512
 FLOPS = 2 * 128 * 9216 * 1024
 
-CV = [512,512,512,512,512,512,512,512,512,512,512,512,512,512,512,512,512,512]
+TAIL = [(0, 512), (512, 768), (768, 1024)]
 AHEAD = 2
 X_GROUPS = [(0, 2, 4, 3, 4, 4), (2, 2, 7, 6, 7, 7), (4, 2, 10, 9, 10, 10), (6, 2, 13, 12, 13, 13), (8, 1, 15, 14, 15, 15)]
 
@@ -112,24 +112,27 @@ def tile_snn_kernel(tc, FF, V, a, Xd, W_int, W_ff, out):
         ]
         raws = {}
 
+        first_lo = keep.tile([P, 4, HALF], BF16)
+        first_hi = keep.tile([P, 4, HALF], BF16)
+
         def w_load(c):
             rows = (
                 w_int_rows[K_PASS * c : K_PASS * (c + 1), :]
                 if c < 16
                 else W_ff[K_PASS * (c - 16) : K_PASS * (c - 15), :]
             ).rearrange("(p t) w -> p t w", t=4)
-            raw = rawp.tile([P, 4, N], BF16, name="raw")
-            raws[c] = raw
             if c == 0:
-                nc.sync.dma_start(out=raw[:, :, HALF:], in_=rows[:, :, HALF:])
-                nc.sync.dma_start(out=raw[:, :, :HALF], in_=rows[:, :, :HALF])
+                nc.sync.dma_start(out=first_hi[:], in_=rows[:, :, HALF:])
+                nc.sync.dma_start(out=first_lo[:], in_=rows[:, :, :HALF])
             else:
+                raw = rawp.tile([P, 4, N], BF16, name="raw")
+                raws[c] = raw
                 nc.sync.dma_start(out=raw[:], in_=rows)
 
-        def regroup(copy, grouped, raw, lo, hi):
+        def regroup(copy, grouped, source, lo, hi):
             copy(
                 out=grouped[:, lo:hi, :].rearrange("p (c i) t -> p c t i", i=4),
-                in_=raw[:, :, lo:hi].rearrange("p t (c i) -> p c t i", i=4),
+                in_=source.rearrange("p t (c i) -> p c t i", i=4),
             )
 
         def quantise(work, lo, hi):
@@ -139,16 +142,16 @@ def tile_snn_kernel(tc, FF, V, a, Xd, W_int, W_ff, out):
                 in_=work[0][:, lo:hi, :].rearrange("p w t -> p (w t)"),
             )
 
-        def multiply(c, h, work):
-            cols = slice(h * HALF, (h + 1) * HALF)
+        def multiply(c, work, lo, hi):
+            cols = slice(lo, hi)
             nc.tensor.matmul_mx(
-                out=acc[h][:],
+                out=acc[lo // HALF][:, lo % HALF : lo % HALF + hi - lo],
                 lhsT=x_codes[:, P * c : P * (c + 1)].bitcast(FP8X4),
                 lhsT_scale=x_scales[:, P * c : P * (c + 1)],
                 rhs=work[1][:, cols].bitcast(FP8X4),
                 rhs_scale=work[2][:, cols],
                 start=(c == 0),
-                stop=(c == PASSES - 1),
+                stop=(c == PASSES - 1 and hi % HALF == 0),
             )
 
         loaded = 0
@@ -163,7 +166,6 @@ def tile_snn_kernel(tc, FF, V, a, Xd, W_int, W_ff, out):
                         x_load(g[0], g[1])
                 w_load(loaded)
                 loaded += 1
-            raw = raws[c]
             for g in X_GROUPS:
                 if g[3] == c:
                     x_transpose(g[0], g[1])
@@ -173,34 +175,40 @@ def tile_snn_kernel(tc, FF, V, a, Xd, W_int, W_ff, out):
             grouped = grpp.tile([P, N, 4], BF16, align_bytes=64)
             codes = codp.tile([P, N], U32, align_bytes=64)
             scales = codp.tile([P, N], U8, align_bytes=64)
-            regroup(nc.scalar.copy, grouped, raw, CV[c], N)
-            regroup(nc.vector.tensor_copy, grouped, raw, 0, CV[c])
+            low = first_lo[:] if c == 0 else raws[c][:, :, :HALF]
+            high = first_hi[:] if c == 0 else raws[c][:, :, HALF:]
+            regroup(nc.scalar.copy, grouped, high, HALF, N)
+            regroup(nc.vector.tensor_copy, grouped, low, 0, HALF)
             for g in X_GROUPS:
                 if g[5] == c:
                     x_quantise(g[0], g[1])
                     x_ready = 2 * (g[0] + g[1])
-            if prev is not None:
+            if c == PASSES - 1:
+                for h in range(2):
+                    quantise(prev, h * HALF, (h + 1) * HALF)
+                    multiply(c - 1, prev, h * HALF, (h + 1) * HALF)
+            elif prev is not None:
                 quantise(prev, 0, N)
                 waiting.append((c - 1, prev))
             while multiplied < len(waiting) and waiting[multiplied][0] < x_ready:
                 job = waiting[multiplied]
-                multiply(job[0], 0, job[1])
-                multiply(job[0], 1, job[1])
+                multiply(job[0], job[1], 0, HALF)
+                multiply(job[0], job[1], HALF, N)
                 multiplied += 1
             prev = (grouped, codes, scales)
-        for h in range(2):
-            quantise(prev, h * HALF, (h + 1) * HALF)
-            multiply(PASSES - 1, h, prev)
+        for lo, hi in TAIL:
+            quantise(prev, lo, hi)
+            multiply(PASSES - 1, prev, lo, hi)
 
         nc.sync.dma_start(out=out[0], in_=spike[:])
         nc.sync.dma_start(out=out[2], in_=a_new[:])
-        for h in range(2):
-            cols = slice(h * HALF, (h + 1) * HALF)
+        for lo, hi in TAIL:
+            cols = slice(lo, hi)
             nc.vector.scalar_tensor_tensor(
                 out=v_new[:, cols],
                 in0=v_keep[:, cols],
                 scalar=0.95,
-                in1=acc[h][:],
+                in1=acc[lo // HALF][:, lo % HALF : lo % HALF + hi - lo],
                 op0=ALU.mult,
                 op1=ALU.add,
             )

@@ -112,22 +112,15 @@ def tile_snn_kernel(tc, FF, V, a, Xd, W_int, W_ff, out):
         ]
         raws = {}
 
-        first_lo = keep.tile([P, 4, HALF], BF16)
-        first_hi = keep.tile([P, 4, HALF], BF16)
-
         def w_load(c):
             rows = (
                 w_int_rows[K_PASS * c : K_PASS * (c + 1), :]
                 if c < 16
                 else W_ff[K_PASS * (c - 16) : K_PASS * (c - 15), :]
             ).rearrange("(p t) w -> p t w", t=4)
-            if c == 0:
-                nc.sync.dma_start(out=first_hi[:], in_=rows[:, :, HALF:])
-                nc.sync.dma_start(out=first_lo[:], in_=rows[:, :, :HALF])
-            else:
-                raw = rawp.tile([P, 4, N], BF16, name="raw")
-                raws[c] = raw
-                nc.sync.dma_start(out=raw[:], in_=rows)
+            raw = rawp.tile([P, 4, N], BF16, name="raw")
+            raws[c] = raw
+            nc.sync.dma_start(out=raw[:], in_=rows)
 
         def regroup(copy, grouped, source, lo, hi):
             copy(
@@ -156,9 +149,13 @@ def tile_snn_kernel(tc, FF, V, a, Xd, W_int, W_ff, out):
 
         loaded = 0
         x_ready = 0
-        waiting = []
-        multiplied = 0
+        jobs = []
         prev = None
+
+        def flush():
+            while jobs and jobs[0][0] < x_ready:
+                multiply(*jobs.pop(0))
+
         for c in range(PASSES):
             while loaded < min(PASSES, c + AHEAD + 1):
                 for g in X_GROUPS:
@@ -175,28 +172,22 @@ def tile_snn_kernel(tc, FF, V, a, Xd, W_int, W_ff, out):
             grouped = grpp.tile([P, N, 4], BF16, align_bytes=64)
             codes = codp.tile([P, N], U32, align_bytes=64)
             scales = codp.tile([P, N], U8, align_bytes=64)
-            low = first_lo[:] if c == 0 else raws[c][:, :, :HALF]
-            high = first_hi[:] if c == 0 else raws[c][:, :, HALF:]
-            regroup(nc.scalar.copy, grouped, high, HALF, N)
-            regroup(nc.vector.tensor_copy, grouped, low, 0, HALF)
+            work = (grouped, codes, scales)
+            regroup(nc.scalar.copy, grouped, raws[c][:, :, HALF:], HALF, N)
+            regroup(nc.vector.tensor_copy, grouped, raws[c][:, :, :HALF], 0, HALF)
             for g in X_GROUPS:
                 if g[5] == c:
                     x_quantise(g[0], g[1])
                     x_ready = 2 * (g[0] + g[1])
-            if c == PASSES - 1:
-                for h in range(2):
-                    quantise(prev, h * HALF, (h + 1) * HALF)
-                    multiply(c - 1, prev, h * HALF, (h + 1) * HALF)
-            elif prev is not None:
-                quantise(prev, 0, N)
-                waiting.append((c - 1, prev))
-            while multiplied < len(waiting) and waiting[multiplied][0] < x_ready:
-                job = waiting[multiplied]
-                multiply(job[0], job[1], 0, HALF)
-                multiply(job[0], job[1], HALF, N)
-                multiplied += 1
-            prev = (grouped, codes, scales)
-        for lo, hi in TAIL:
+            if prev is not None:
+                quantise(prev, HALF, N)
+                jobs.append((c - 1, prev, HALF, N))
+                flush()
+            quantise(work, 0, HALF)
+            jobs.append((c, work, 0, HALF))
+            flush()
+            prev = work
+        for lo, hi in TAIL[1:]:
             quantise(prev, lo, hi)
             multiply(PASSES - 1, prev, lo, hi)
 

@@ -19,6 +19,7 @@ HALF = 512
 FLOPS = 2 * 128 * 9216 * 1024
 
 TAIL = [(0, 512), (512, 768), (768, 1024)]
+V_LAST = 416
 AHEAD = 2
 X_GROUPS = [(0, 2, 4, 3, 4, 4), (2, 2, 7, 6, 7, 7), (4, 2, 10, 9, 10, 10), (6, 2, 13, 12, 13, 13), (8, 1, 15, 14, 15, 15)]
 
@@ -50,17 +51,18 @@ def tile_snn_kernel(tc, FF, V, a, Xd, W_int, W_ff, out):
         theta = keep.tile([P, N], F32)
         spike = keep.tile([P, N], F32)
         a_new = keep.tile([P, N], F32)
-        v_keep = keep.tile([P, N], F32)
+        quiet = keep.tile([P, N], BF16)
+        v_keep = keep.tile([P, N], BF16)
         v_new = keep.tile([P, N], F32)
-        for h in range(2):
-            cols = slice(h * HALF, (h + 1) * HALF)
+        halves = [slice(0, HALF), slice(HALF, N)]
+        for cols in halves:
             nc.scalar.activation(out=theta[:, cols], in_=a_sb[:, cols], func=ACT.Copy, scale=1.8, bias=1.0)
-            nc.vector.tensor_tensor(out=spike[:, cols], in0=v_sb[:, cols], in1=theta[:, cols], op=ALU.is_gt)
+        for cols in halves:
+            nc.vector.tensor_tensor(out=quiet[:, cols], in0=v_sb[:, cols], in1=theta[:, cols], op=ALU.is_le)
+            nc.scalar.activation(out=spike[:, cols], in_=quiet[:, cols], func=ACT.Copy, scale=-1.0, bias=1.0)
+        nc.vector.tensor_tensor(out=v_keep[:], in0=quiet[:], in1=v_sb[:], op=ALU.mult)
         nc.vector.scalar_tensor_tensor(
             out=a_new[:], in0=a_sb[:], scalar=0.9, in1=spike[:], op0=ALU.mult, op1=ALU.add
-        )
-        nc.vector.scalar_tensor_tensor(
-            out=v_keep[:], in0=spike[:], scalar=0.0, in1=v_sb[:], op0=ALU.is_equal, op1=ALU.mult
         )
 
         x32 = x_sb[:].bitcast(F32)
@@ -173,8 +175,11 @@ def tile_snn_kernel(tc, FF, V, a, Xd, W_int, W_ff, out):
             codes = codp.tile([P, N], U32, align_bytes=64)
             scales = codp.tile([P, N], U8, align_bytes=64)
             work = (grouped, codes, scales)
-            regroup(nc.scalar.copy, grouped, raws[c][:, :, HALF:], HALF, N)
-            regroup(nc.vector.tensor_copy, grouped, raws[c][:, :, :HALF], 0, HALF)
+            last = c == PASSES - 1
+            v_cols = V_LAST if last else HALF
+            for lo, hi in [(V_LAST, HALF)] + TAIL[1:] if last else [(HALF, N)]:
+                regroup(nc.scalar.copy, grouped, raws[c][:, :, lo:hi], lo, hi)
+            regroup(nc.vector.tensor_copy, grouped, raws[c][:, :, :v_cols], 0, v_cols)
             for g in X_GROUPS:
                 if g[5] == c:
                     x_quantise(g[0], g[1])

from contextlib import ExitStack

import concourse.mybir as mybir
from concourse.masks import make_identity

FP8X4 = mybir.dt.float8_e4m3fn_x4
BF16 = mybir.dt.bfloat16
F32 = mybir.dt.float32
U32 = mybir.dt.uint32
U8 = mybir.dt.uint8
ALU = mybir.AluOpType
ACT = mybir.ActivationFunctionType

P = 128
N = 1024
K_PASS = 512
PASSES = 18
HALF = 512
FLOPS = 2 * 128 * 9216 * 1024

TAIL = [(0, 512), (512, 768), (768, 1024)]
V_LAST = 416
AHEAD = 2
X_GROUPS = [(0, 2, 4, 3, 4, 4), (2, 2, 7, 6, 7, 7), (4, 2, 10, 9, 10, 10), (6, 2, 13, 12, 13, 13), (8, 1, 15, 14, 15, 15)]


def tile_snn_kernel(tc, FF, V, a, Xd, W_int, W_ff, out):
    nc = tc.nc
    w_int_rows = W_int.rearrange("d n m -> (d n) m")
    with ExitStack() as ctx:
        keep = ctx.enter_context(tc.tile_pool(name="keep", bufs=1))
        rawp = ctx.enter_context(tc.tile_pool(name="rawp", bufs=8))
        grpp = ctx.enter_context(tc.tile_pool(name="grpp", bufs=4))
        codp = ctx.enter_context(tc.tile_pool(name="codp", bufs=8))
        psx = ctx.enter_context(tc.psum_pool(name="psx", bufs=4))
        psa = ctx.enter_context(tc.psum_pool(name="psa", bufs=1))
        ctx.enter_context(tc.manual_schedule())

        ident = keep.tile([P, P], F32)
        make_identity(nc, ident[:])

        warm = keep.tile([P, 1], F32)
        nc.scalar.copy(out=warm[:], in_=ident[:, 0:1])

        a_sb = keep.tile([P, N], BF16)
        v_sb = keep.tile([P, N], BF16)
        x_sb = keep.tile([P, 9 * N], BF16)
        nc.sync.dma_start(out=a_sb[:], in_=a)
        nc.sync.dma_start(out=v_sb[:], in_=V)

        theta = keep.tile([P, N], F32)
        spike = keep.tile([P, N], F32)
        a_new = keep.tile([P, N], F32)
        quiet = keep.tile([P, N], BF16)
        v_keep = keep.tile([P, N], BF16)
        v_new = keep.tile([P, N], F32)
        halves = [slice(0, HALF), slice(HALF, N)]
        for cols in halves:
            nc.scalar.activation(out=theta[:, cols], in_=a_sb[:, cols], func=ACT.Copy, scale=1.8, bias=1.0)
        for cols in halves:
            nc.vector.tensor_tensor(out=quiet[:, cols], in0=v_sb[:, cols], in1=theta[:, cols], op=ALU.is_le)
            nc.scalar.activation(out=spike[:, cols], in_=quiet[:, cols], func=ACT.Copy, scale=-1.0, bias=1.0)
        nc.vector.tensor_tensor(out=v_keep[:], in0=quiet[:], in1=v_sb[:], op=ALU.mult)
        nc.vector.scalar_tensor_tensor(
            out=a_new[:], in0=a_sb[:], scalar=0.9, in1=spike[:], op0=ALU.mult, op1=ALU.add
        )

        x32 = x_sb[:].bitcast(F32)
        xg = keep.tile([P, PASSES * P * 4], BF16, align_bytes=64)
        xg32 = xg[:].bitcast(F32)
        x_codes = keep.tile([P, PASSES * P], U32, align_bytes=64)
        x_scales = keep.tile([P, PASSES * P], U8, align_bytes=64)
        x_banks = {}

        def x_load(d0, nd):
            if d0 == 8:
                nc.sync.dma_start(out=x_sb[:, 8 * N : 9 * N], in_=FF)
            else:
                nc.sync.dma_start(
                    out=x_sb[:, d0 * N : (d0 + nd) * N].rearrange("b (d n) -> b d n", d=nd),
                    in_=Xd[d0 : d0 + nd].rearrange("d b n -> b d n"),
                )

        def x_transpose(d0, nd):
            for d in range(d0, d0 + nd):
                xt = psx.tile([P, 2, 2, P], F32, name="xt")
                x_banks[d] = xt
                for j in range(2):
                    c = 2 * d + j
                    for u in range(2):
                        nc.tensor.transpose(
                            xt[:, j, u, :], x32[:, 256 * c + u : 256 * (c + 1) : 2], ident[:]
                        )

        def x_copy(d0, nd):
            for d in range(d0, d0 + nd):
                nc.scalar.copy(
                    out=xg32[:, 512 * d : 512 * (d + 1)].rearrange(
                        "p (j b u) -> p j b u", j=2, u=2
                    ),
                    in_=x_banks[d][:].rearrange("p j u b -> p j b u"),
                )

        def x_quantise(d0, nd):
            nc.vector.quantize_mx(
                out=x_codes[:, 256 * d0 : 256 * (d0 + nd)].bitcast(FP8X4),
                scales=x_scales[:, 256 * d0 : 256 * (d0 + nd)],
                in_=xg[:, 1024 * d0 : 1024 * (d0 + nd)],
            )

        acc = [
            psa.tile([P, HALF], F32, name="acc0"),
            psa.tile([P, HALF], F32, name="acc1"),
        ]
        raws = {}

        def w_load(c):
            rows = (
                w_int_rows[K_PASS * c : K_PASS * (c + 1), :]
                if c < 16
                else W_ff[K_PASS * (c - 16) : K_PASS * (c - 15), :]
            ).rearrange("(p t) w -> p t w", t=4)
            raw = rawp.tile([P, 4, N], BF16, name="raw")
            raws[c] = raw
            nc.sync.dma_start(out=raw[:], in_=rows)

        def regroup(copy, grouped, source, lo, hi):
            copy(
                out=grouped[:, lo:hi, :].rearrange("p (c i) t -> p c t i", i=4),
                in_=source.rearrange("p t (c i) -> p c t i", i=4),
            )

        def quantise(work, lo, hi):
            nc.vector.quantize_mx(
                out=work[1][:, lo:hi].bitcast(FP8X4),
                scales=work[2][:, lo:hi],
                in_=work[0][:, lo:hi, :].rearrange("p w t -> p (w t)"),
            )

        def multiply(c, work, lo, hi):
            cols = slice(lo, hi)
            nc.tensor.matmul_mx(
                out=acc[lo // HALF][:, lo % HALF : lo % HALF + hi - lo],
                lhsT=x_codes[:, P * c : P * (c + 1)].bitcast(FP8X4),
                lhsT_scale=x_scales[:, P * c : P * (c + 1)],
                rhs=work[1][:, cols].bitcast(FP8X4),
                rhs_scale=work[2][:, cols],
                start=(c == 0),
                stop=(c == PASSES - 1 and hi % HALF == 0),
            )

        loaded = 0
        x_ready = 0
        jobs = []
        prev = None

        def flush():
            while jobs and jobs[0][0] < x_ready:
                multiply(*jobs.pop(0))

        for c in range(PASSES):
            while loaded < min(PASSES, c + AHEAD + 1):
                for g in X_GROUPS:
                    if g[2] == loaded:
                        x_load(g[0], g[1])
                w_load(loaded)
                loaded += 1
            for g in X_GROUPS:
                if g[3] == c:
                    x_transpose(g[0], g[1])
            for g in X_GROUPS:
                if g[4] == c:
                    x_copy(g[0], g[1])
            grouped = grpp.tile([P, N, 4], BF16, align_bytes=64)
            codes = codp.tile([P, N], U32, align_bytes=64)
            scales = codp.tile([P, N], U8, align_bytes=64)
            work = (grouped, codes, scales)
            last = c == PASSES - 1
            v_cols = V_LAST if last else HALF
            for lo, hi in [(V_LAST, HALF)] + TAIL[1:] if last else [(HALF, N)]:
                regroup(nc.scalar.copy, grouped, raws[c][:, :, lo:hi], lo, hi)
            regroup(nc.vector.tensor_copy, grouped, raws[c][:, :, :v_cols], 0, v_cols)
            for g in X_GROUPS:
                if g[5] == c:
                    x_quantise(g[0], g[1])
                    x_ready = 2 * (g[0] + g[1])
            if prev is not None:
                quantise(prev, HALF, N)
                jobs.append((c - 1, prev, HALF, N))
                flush()
            quantise(work, 0, HALF)
            jobs.append((c, work, 0, HALF))
            flush()
            prev = work
        for lo, hi in TAIL[1:]:
            quantise(prev, lo, hi)
            multiply(PASSES - 1, prev, lo, hi)

        nc.sync.dma_start(out=out[0], in_=spike[:])
        nc.sync.dma_start(out=out[2], in_=a_new[:])
        for lo, hi in TAIL:
            cols = slice(lo, hi)
            nc.vector.scalar_tensor_tensor(
                out=v_new[:, cols],
                in0=v_keep[:, cols],
                scalar=0.95,
                in1=acc[lo // HALF][:, lo % HALF : lo % HALF + hi - lo],
                op0=ALU.mult,
                op1=ALU.add,
            )
            nc.sync.dma_start(out=out[1][:, cols], in_=v_new[:, cols])
